import numpy as np
import ml_dtypes


def mxq(x, axis, fmt="e4m3"):
    dtype, down = {"e4m3": (ml_dtypes.float8_e4m3fn, 7), "e5m2": (ml_dtypes.float8_e5m2, 14)}[fmt]
    v = np.moveaxis(np.asarray(x, np.float32).astype(ml_dtypes.bfloat16).astype(np.float64), axis, -1)
    blocks = v.reshape(v.shape[:-1] + (-1, 32))
    amax = np.abs(blocks).max(-1, keepdims=True)
    byte = np.maximum(np.where(amax > 0, np.frexp(amax)[1] - 1 + 127, 0) - down, 1)
    scale = np.exp2(byte - 127.0)
    codes = (blocks / scale).astype(np.float32).astype(dtype).astype(np.float64)
    return np.moveaxis((codes * scale).reshape(v.shape), -1, axis)


WIDE = False


def mx_kscale(k):
    if not WIDE:
        return np.ones(k)
    levels = np.array([10, -10, 5, -5, 0])
    a = np.random.permutation(np.resize(levels, k // 512 * 4)).reshape(k // 512, 4)
    idx = np.arange(k)
    return np.exp2(a[idx // 512, idx % 128 // 32])


BF16 = ml_dtypes.bfloat16


def bf(x):
    return np.asarray(x, np.float32).astype(BF16)


def f64(x):
    return np.asarray(x).astype(np.float64)


B, HID, UD = 4096, 512, 512


def sigmoid(v):
    return 1.0 / (1.0 + np.exp(-v))


def setup_inputs():
    s, u = mx_kscale(HID), mx_kscale(UD)
    return {
        "encoder_hidden": bf(np.random.standard_normal((B, HID)) * s),
        "spk_vectors": bf(np.random.standard_normal((B, UD))),
        "adr_vectors": bf(np.random.standard_normal((B, UD)) * u),
        "h_tilde": bf(np.tanh(np.random.standard_normal((B, UD)) * 1.3)),
        "WA_xz": bf(np.random.standard_normal((UD, HID)) / np.sqrt(HID) / s),
        "WA_hz": bf(np.random.standard_normal((UD, UD)) / np.sqrt(UD)),
        "VA_hz": bf(np.random.standard_normal((UD, UD)) / np.sqrt(UD) / u),
    }


def reference(encoder_hidden, spk_vectors, adr_vectors, h_tilde, WA_xz, WA_hz, VA_hz):
    x, hs, ha = f64(encoder_hidden), f64(spk_vectors), f64(adr_vectors)
    z_t = sigmoid((mxq(x, 1, "e4m3") @ mxq(f64(WA_xz), 1, "e4m3").T)
                  + (mxq(hs, 1, "e4m3") @ mxq(f64(WA_hz), 1, "e4m3").T)
                  + (mxq(ha, 1, "e4m3") @ mxq(f64(VA_hz), 1, "e4m3").T))
    return (1.0 - z_t) * hs + z_t * f64(h_tilde)

@@ -1,0 +1,210 @@
+from contextlib import ExitStack
+
+import concourse.mybir as mybir
+from concourse.masks import make_identity
+
+F32 = mybir.dt.float32
+BF16 = mybir.dt.bfloat16
+U32 = mybir.dt.uint32
+U8 = mybir.dt.uint8
+FP8X4 = mybir.dt.float8_e4m3fn_x4
+ALU = mybir.AluOpType
+ACT = mybir.ActivationFunctionType
+
+P = 128
+B, K, N = 4096, 512, 512
+NT = B // P
+GT = 2
+NG = NT // GT
+KW = K // 2
+FLOPS = 2 * B * N * 3 * K
+
+CHUNKS = [2, 2, 4, 4, 4, 4, 4, 4, 4]
+AHEAD = 4
+PINNED = True
+H_GROUPS = list(range(NG))
+
+
+def tile_updatespeaker_pc_t_kernel(tc, encoder_hidden, spk_vectors, adr_vectors, h_tilde,
+                                              WA_xz, WA_hz, VA_hz, out):
+    nc = tc.nc
+    acts = [encoder_hidden, spk_vectors, adr_vectors, h_tilde]
+    weights = [WA_xz, WA_hz, VA_hz]
+    chunk_start = [sum(CHUNKS[:c]) for c in range(len(CHUNKS))]
+    chunk_of_tile = {}
+    for c, n in enumerate(CHUNKS):
+        for t in range(chunk_start[c], chunk_start[c] + n):
+            chunk_of_tile[t] = c
+
+    with ExitStack() as ctx:
+        keep = ctx.enter_context(tc.tile_pool(name="keep", bufs=1))
+        wgrp_pool = ctx.enter_context(tc.tile_pool(name="wgrp", bufs=3))
+        grp_pool = ctx.enter_context(tc.tile_pool(name="grp", bufs=9))
+        cod_pool = ctx.enter_context(tc.tile_pool(name="cod", bufs=9))
+        z_pool = ctx.enter_context(tc.tile_pool(name="zp", bufs=3))
+        d_pool = ctx.enter_context(tc.tile_pool(name="dp", bufs=4))
+        tp_pool = ctx.enter_context(tc.psum_pool(name="tp", bufs=4))
+        v_pool = ctx.enter_context(tc.psum_pool(name="vp", bufs=2))
+        h_pool = ctx.enter_context(tc.psum_pool(name="hp", bufs=2))
+        if PINNED:
+            ctx.enter_context(tc.manual_schedule())
+
+        warm_in = keep.tile([P, 1], F32, name="warm_in")
+        warm_out = keep.tile([P, 1], F32, name="warm_out")
+        nc.vector.memset(warm_in[:], 0.0)
+        nc.scalar.activation(out=warm_out[:], in_=warm_in[:], func=ACT.Sigmoid)
+        ident_f = keep.tile([P, P], F32, name="ident_f")
+        make_identity(nc, ident_f[:])
+        ident_b = keep.tile([P, P], BF16, name="ident_b")
+        make_identity(nc, ident_b[:])
+
+        act_tiles = {}
+
+        def load_chunk(a, c):
+            n = CHUNKS[c]
+            t0 = chunk_start[c]
+            sb = keep.tile([P, n * K], BF16, name="in%d_%d" % (a, c))
+            src = acts[a].rearrange("(p t) k -> p (t k)", t=NT)
+            nc.sync.dma_start(out=sb[:], in_=src[:, t0 * K:(t0 + n) * K])
+            act_tiles[(a, c)] = sb
+
+        def act_cols(a, t, n_tiles):
+            c = chunk_of_tile[t]
+            off = (t - chunk_start[c]) * K
+            return act_tiles[(a, c)][:, off:off + n_tiles * K]
+
+        wraw = []
+
+        def load_weight(w):
+            sb = keep.tile([P, 4 * K], BF16, name="wraw%d" % w)
+            nc.sync.dma_start(out=sb[:].rearrange("p (j k) -> p j k", j=4),
+                              in_=weights[w].rearrange("(j p) k -> p j k", p=P))
+            wraw.append(sb)
+
+        def transpose_pair(src2):
+            words = src2.bitcast(F32)
+            bank = tp_pool.tile([P, GT, 2, P], F32, name="bank", tag="bank")
+            for j in range(GT):
+                for u in range(2):
+                    lo = j * KW + u * P
+                    nc.tensor.transpose(bank[:, j, u, :], words[:, lo:lo + P], ident_f[:])
+            return bank
+
+        def evacuate(engine, dst_bf16, bank):
+            dst = dst_bf16.bitcast(F32).rearrange("p (j r u) -> p j r u", j=GT, u=2)
+            src = bank[:].rearrange("p j u r -> p j r u")
+            if engine == "act":
+                nc.scalar.copy(out=dst, in_=src)
+            else:
+                nc.vector.tensor_copy(out=dst, in_=src)
+
+        w_codes, w_scales, w_grp = [], [], []
+
+        def weight_transposes(w):
+            grp = wgrp_pool.tile([P, 4 * N], BF16, name="wgrp", tag="wgrp", align_bytes=64)
+            w_grp.append(grp)
+            for half in range(2):
+                bank = transpose_pair(wraw[w][:, half * 2 * K:(half + 1) * 2 * K])
+                evacuate("dve" if half == 0 else "act", grp[:, half * 2 * N:(half + 1) * 2 * N], bank)
+
+        def weight_quantise(w):
+            codes = keep.tile([P, N], U32, name="wcod%d" % w, align_bytes=64)
+            scales = keep.tile([P, N], U8, name="wscl%d" % w, align_bytes=64)
+            nc.vector.quantize_mx(out=codes[:].bitcast(FP8X4), scales=scales[:], in_=w_grp[w][:])
+            w_codes.append(codes)
+            w_scales.append(scales)
+
+        grp_tiles, cod_tiles = {}, {}
+
+        def act_transposes(g, a):
+            bank = transpose_pair(act_cols(a, g * GT, GT))
+            grp = grp_pool.tile([P, GT * P * 4], BF16, name="grp", tag="grp", align_bytes=64)
+            evacuate("act", grp[:], bank)
+            grp_tiles[(g, a)] = grp
+
+        def act_quantise(g, a):
+            codes = cod_pool.tile([P, GT * P], U32, name="cod", tag="cod", align_bytes=64)
+            scales = cod_pool.tile([P, GT * P], U8, name="scl", tag="scl", align_bytes=64)
+            nc.vector.quantize_mx(out=codes[:].bitcast(FP8X4), scales=scales[:], in_=grp_tiles[(g, a)][:])
+            cod_tiles[(g, a)] = (codes, scales)
+
+        hb_tiles, v_tiles, z_tiles, d_tiles = {}, {}, {}, {}
+
+        def hs_to_psum(g):
+            hb = h_pool.tile([P, GT * N], BF16, name="hb", tag="hb")
+            for j in range(GT):
+                nc.tensor.matmul(hb[:, j * N:(j + 1) * N], lhsT=ident_b[:], rhs=act_cols(1, g * GT + j, 1),
+                                 start=True, stop=True)
+            hb_tiles[g] = hb
+
+        def products(g):
+            for j in range(GT):
+                v = v_pool.tile([P, N], F32, name="v", tag="v")
+                for a in range(3):
+                    codes, scales = cod_tiles[(g, a)]
+                    nc.tensor.matmul_mx(out=v[:],
+                                        lhsT=codes[:, j * P:(j + 1) * P].bitcast(FP8X4),
+                                        lhsT_scale=scales[:, j * P:(j + 1) * P],
+                                        rhs=w_codes[a][:].bitcast(FP8X4),
+                                        rhs_scale=w_scales[a][:],
+                                        start=(a == 0), stop=(a == 2))
+                v_tiles[(g, j)] = v
+
+        def hs_operand(g):
+            return hb_tiles[g][:] if g in H_GROUPS else act_cols(1, g * GT, GT)
+
+        def difference(g):
+            d = d_pool.tile([P, GT * N], F32, name="d", tag="d")
+            nc.vector.tensor_tensor(out=d[:], in0=act_cols(3, g * GT, GT), in1=hs_operand(g), op=ALU.subtract)
+            d_tiles[g] = d
+
+        def gate(g):
+            z = z_pool.tile([P, GT * N], F32, name="z", tag="z")
+            for j in range(GT):
+                nc.scalar.activation(out=z[:, j * N:(j + 1) * N], in_=v_tiles[(g, j)][:], func=ACT.Sigmoid)
+            z_tiles[g] = z
+
+        def scale_difference(g):
+            eng = nc.gpsimd if g in H_GROUPS else nc.vector
+            eng.tensor_tensor(out=d_tiles[g][:], in0=z_tiles[g][:], in1=d_tiles[g][:], op=ALU.mult)
+
+        def finish(g):
+            d = d_tiles[g]
+            nc.vector.tensor_tensor(out=d[:], in0=d[:], in1=hs_operand(g), op=ALU.add)
+            dst = out.rearrange("(p t) n -> p (t n)", t=NT)
+            nc.sync.dma_start(out=dst[:, g * GT * N:(g + 1) * GT * N], in_=d[:])
+
+        first_chunks = [c for c in range(len(CHUNKS)) if chunk_start[c] < AHEAD * GT]
+        for a in range(3):
+            load_chunk(a, 0)
+            load_weight(a)
+        load_chunk(3, 0)
+        for c in first_chunks[1:]:
+            for a in range(4):
+                load_chunk(a, c)
+        for a in range(3):
+            act_transposes(0, a)
+            weight_transposes(a)
+            act_quantise(0, a)
+            weight_quantise(a)
+
+        for i in range(NG):
+            t_next = (i + AHEAD) * GT
+            if t_next < NT and chunk_start[chunk_of_tile[t_next]] == t_next:
+                for a in range(4):
+                    load_chunk(a, chunk_of_tile[t_next])
+            if i + 1 < NG:
+                for a in range(3):
+                    act_transposes(i + 1, a)
+            if i in H_GROUPS:
+                hs_to_psum(i)
+            products(i)
+            difference(i)
+            if i + 1 < NG:
+                for a in range(3):
+                    act_quantise(i + 1, a)
+            gate(i)
+            if i >= 1:
+                finish(i - 1)
+            scale_difference(i)
+        finish(NG - 1)

@@ -22,7 +22,7 @@ FLOPS = 2 * B * N * 3 * K
 CHUNKS = [2, 2, 4, 4, 4, 4, 4, 4, 4]
 AHEAD = 4
 PINNED = True
-H_GROUPS = list(range(NG))
+H_GROUPS = []
 
 
 def tile_updatespeaker_pc_t_kernel(tc, encoder_hidden, spk_vectors, adr_vectors, h_tilde,

@@ -19,10 +19,10 @@ NG = NT // GT
 KW = K // 2
 FLOPS = 2 * B * N * 3 * K
 
-CHUNKS = [2, 2, 4, 4, 4, 4, 4, 4, 4]
-AHEAD = 4
+CHUNKS = [2, 2, 2, 2, 4, 4, 4, 4, 4, 4]
+AHEAD = 7
 PINNED = True
-H_GROUPS = []
+H_GROUPS = list(range(NG))
 
 
 def tile_updatespeaker_pc_t_kernel(tc, encoder_hidden, spk_vectors, adr_vectors, h_tilde,
@@ -39,13 +39,13 @@ def tile_updatespeaker_pc_t_kernel(tc, encoder_hidden, spk_vectors, adr_vectors,
     with ExitStack() as ctx:
         keep = ctx.enter_context(tc.tile_pool(name="keep", bufs=1))
         wgrp_pool = ctx.enter_context(tc.tile_pool(name="wgrp", bufs=3))
-        grp_pool = ctx.enter_context(tc.tile_pool(name="grp", bufs=9))
-        cod_pool = ctx.enter_context(tc.tile_pool(name="cod", bufs=9))
+        grp_pool = ctx.enter_context(tc.tile_pool(name="grp", bufs=6))
+        cod_pool = ctx.enter_context(tc.tile_pool(name="cod", bufs=6))
         z_pool = ctx.enter_context(tc.tile_pool(name="zp", bufs=3))
-        d_pool = ctx.enter_context(tc.tile_pool(name="dp", bufs=4))
-        tp_pool = ctx.enter_context(tc.psum_pool(name="tp", bufs=4))
+        d_pool = ctx.enter_context(tc.tile_pool(name="dp", bufs=8))
+        tp_pool = ctx.enter_context(tc.psum_pool(name="tp", bufs=3))
         v_pool = ctx.enter_context(tc.psum_pool(name="vp", bufs=2))
-        h_pool = ctx.enter_context(tc.psum_pool(name="hp", bufs=2))
+        h_pool = ctx.enter_context(tc.psum_pool(name="hp", bufs=3))
         if PINNED:
             ctx.enter_context(tc.manual_schedule())
 
@@ -174,37 +174,68 @@ def tile_updatespeaker_pc_t_kernel(tc, encoder_hidden, spk_vectors, adr_vectors,
             dst = out.rearrange("(p t) n -> p (t n)", t=NT)
             nc.sync.dma_start(out=dst[:, g * GT * N:(g + 1) * GT * N], in_=d[:])
 
-        first_chunks = [c for c in range(len(CHUNKS)) if chunk_start[c] < AHEAD * GT]
-        for a in range(3):
-            load_chunk(a, 0)
-            load_weight(a)
-        load_chunk(3, 0)
-        for c in first_chunks[1:]:
-            for a in range(4):
+        def last_group_by_tile(g):
+            dst = out.rearrange("(p t) n -> p (t n)", t=NT)
+            parts = []
+            for j in range(GT):
+                dj = d_pool.tile([P, N], F32, name="d", tag="d")
+                nc.vector.tensor_tensor(out=dj[:], in0=act_cols(3, g * GT + j, 1), in1=hb_tiles[g][:, j * N:(j + 1) * N],
+                                        op=ALU.subtract)
+                parts.append(dj)
+            zs = []
+            for j in range(GT):
+                zj = z_pool.tile([P, N], F32, name="z", tag="z")
+                nc.scalar.activation(out=zj[:], in_=v_tiles[(g, j)][:], func=ACT.Sigmoid)
+                zs.append(zj)
+            finish(g - 1)
+            for j in range(GT):
+                dj = parts[j]
+                nc.vector.tensor_tensor(out=dj[:], in0=zs[j][:], in1=dj[:], op=ALU.mult)
+                nc.vector.tensor_tensor(out=dj[:], in0=dj[:], in1=hb_tiles[g][:, j * N:(j + 1) * N], op=ALU.add)
+                t = g * GT + j
+                nc.sync.dma_start(out=dst[:, t * N:(t + 1) * N], in_=dj[:])
+
+        load_order = []
+        for c in range(len(CHUNKS)):
+            for a in range(3):
+                load_order.append((a, c))
+            if c >= 1:
+                load_order.append((3, c - 1))
+        load_order.append((3, len(CHUNKS) - 1))
+        issued = [0]
+
+        def issue_loads_up_to(g):
+            while issued[0] < len(load_order):
+                a, c = load_order[issued[0]]
+                if chunk_start[c] > g * GT:
+                    break
                 load_chunk(a, c)
+                issued[0] += 1
+
+        for w in range(3):
+            load_weight(w)
+        issue_loads_up_to(AHEAD - 1)
+        for w in range(3):
+            weight_transposes(w)
+            weight_quantise(w)
         for a in range(3):
             act_transposes(0, a)
-            weight_transposes(a)
+        for a in range(3):
             act_quantise(0, a)
-            weight_quantise(a)
 
-        for i in range(NG):
-            t_next = (i + AHEAD) * GT
-            if t_next < NT and chunk_start[chunk_of_tile[t_next]] == t_next:
-                for a in range(4):
-                    load_chunk(a, chunk_of_tile[t_next])
-            if i + 1 < NG:
-                for a in range(3):
-                    act_transposes(i + 1, a)
-            if i in H_GROUPS:
-                hs_to_psum(i)
+        for i in range(NG - 1):
+            issue_loads_up_to(i + AHEAD)
+            for a in range(3):
+                act_transposes(i + 1, a)
+            hs_to_psum(i)
             products(i)
             difference(i)
-            if i + 1 < NG:
-                for a in range(3):
-                    act_quantise(i + 1, a)
+            for a in range(3):
+                act_quantise(i + 1, a)
             gate(i)
             if i >= 1:
                 finish(i - 1)
             scale_difference(i)
-        finish(NG - 1)
+        hs_to_psum(NG - 1)
+        products(NG - 1)
+        last_group_by_tile(NG - 1)

@@ -130,12 +130,12 @@ def tile_updatespeaker_pc_t_kernel(tc, encoder_hidden, spk_vectors, adr_vectors,
 
         hb_tiles, v_tiles, z_tiles, d_tiles = {}, {}, {}, {}
 
-        def hs_to_psum(g):
-            hb = h_pool.tile([P, GT * N], BF16, name="hb", tag="hb")
-            for j in range(GT):
-                nc.tensor.matmul(hb[:, j * N:(j + 1) * N], lhsT=ident_b[:], rhs=act_cols(1, g * GT + j, 1),
-                                 start=True, stop=True)
-            hb_tiles[g] = hb
+        def hs_to_psum(g, j):
+            if j == 0:
+                hb = h_pool.tile([P, GT * N], BF16, name="hb", tag="hb")
+                hb_tiles[g] = hb
+            nc.tensor.matmul(hb_tiles[g][:, j * N:(j + 1) * N], lhsT=ident_b[:], rhs=act_cols(1, g * GT + j, 1),
+                             start=True, stop=True)
 
         def products(g):
             for j in range(GT):
@@ -223,12 +223,14 @@ def tile_updatespeaker_pc_t_kernel(tc, encoder_hidden, spk_vectors, adr_vectors,
         for a in range(3):
             act_quantise(0, a)
 
+        hs_to_psum(0, 0)
         for i in range(NG - 1):
             issue_loads_up_to(i + AHEAD)
             for a in range(3):
                 act_transposes(i + 1, a)
-            hs_to_psum(i)
+            hs_to_psum(i, 1)
             products(i)
+            hs_to_psum(i + 1, 0)
             difference(i)
             for a in range(3):
                 act_quantise(i + 1, a)
@@ -236,6 +238,6 @@ def tile_updatespeaker_pc_t_kernel(tc, encoder_hidden, spk_vectors, adr_vectors,
             if i >= 1:
                 finish(i - 1)
             scale_difference(i)
-        hs_to_psum(NG - 1)
+        hs_to_psum(NG - 1, 1)
         products(NG - 1)
         last_group_by_tile(NG - 1)

@@ -77,8 +77,7 @@ def tile_updatespeaker_pc_t_kernel(tc, encoder_hidden, spk_vectors, adr_vectors,
 
         def load_weight(w):
             sb = keep.tile([P, 4 * K], BF16, name="wraw%d" % w)
-            nc.sync.dma_start(out=sb[:].rearrange("p (j k) -> p j k", j=4),
-                              in_=weights[w].rearrange("(j p) k -> p j k", p=P))
+            nc.sync.dma_start(out=sb[:], in_=weights[w].rearrange("(p j) k -> p (j k)", j=4))
             wraw.append(sb)
 
         def transpose_pair(src2):
@@ -90,9 +89,7 @@ def tile_updatespeaker_pc_t_kernel(tc, encoder_hidden, spk_vectors, adr_vectors,
                     nc.tensor.transpose(bank[:, j, u, :], words[:, lo:lo + P], ident_f[:])
             return bank
 
-        def evacuate(engine, dst_bf16, bank):
-            dst = dst_bf16.bitcast(F32).rearrange("p (j r u) -> p j r u", j=GT, u=2)
-            src = bank[:].rearrange("p j u r -> p j r u")
+        def evacuate(engine, dst, src):
             if engine == "act":
                 nc.scalar.copy(out=dst, in_=src)
             else:
@@ -103,9 +100,10 @@ def tile_updatespeaker_pc_t_kernel(tc, encoder_hidden, spk_vectors, adr_vectors,
         def weight_transposes(w):
             grp = wgrp_pool.tile([P, 4 * N], BF16, name="wgrp", tag="wgrp", align_bytes=64)
             w_grp.append(grp)
+            by_half = grp[:].bitcast(F32).rearrange("p (r h j u) -> p h r j u", h=2, j=2, u=2)
             for half in range(2):
                 bank = transpose_pair(wraw[w][:, half * 2 * K:(half + 1) * 2 * K])
-                evacuate("dve" if half == 0 else "act", grp[:, half * 2 * N:(half + 1) * 2 * N], bank)
+                evacuate("act" if w == 1 else "dve", by_half[:, half], bank[:].rearrange("p j u r -> p r j u"))
 
         def weight_quantise(w):
             codes = keep.tile([P, N], U32, name="wcod%d" % w, align_bytes=64)
@@ -119,7 +117,8 @@ def tile_updatespeaker_pc_t_kernel(tc, encoder_hidden, spk_vectors, adr_vectors,
         def act_transposes(g, a):
             bank = transpose_pair(act_cols(a, g * GT, GT))
             grp = grp_pool.tile([P, GT * P * 4], BF16, name="grp", tag="grp", align_bytes=64)
-            evacuate("act", grp[:], bank)
+            evacuate("act", grp[:].bitcast(F32).rearrange("p (j r u) -> p j r u", j=GT, u=2),
+                     bank[:].rearrange("p j u r -> p j r u"))
             grp_tiles[(g, a)] = grp
 
         def act_quantise(g, a):
@@ -187,10 +186,11 @@ def tile_updatespeaker_pc_t_kernel(tc, encoder_hidden, spk_vectors, adr_vectors,
                 zj = z_pool.tile([P, N], F32, name="z", tag="z")
                 nc.scalar.activation(out=zj[:], in_=v_tiles[(g, j)][:], func=ACT.Sigmoid)
                 zs.append(zj)
+            nc.gpsimd.tensor_tensor(out=parts[0][:], in0=zs[0][:], in1=parts[0][:], op=ALU.mult)
             finish(g - 1)
+            nc.vector.tensor_tensor(out=parts[1][:], in0=zs[1][:], in1=parts[1][:], op=ALU.mult)
             for j in range(GT):
                 dj = parts[j]
-                nc.vector.tensor_tensor(out=dj[:], in0=zs[j][:], in1=dj[:], op=ALU.mult)
                 nc.vector.tensor_tensor(out=dj[:], in0=dj[:], in1=hb_tiles[g][:, j * N:(j + 1) * N], op=ALU.add)
                 t = g * GT + j
                 nc.sync.dma_start(out=dst[:, t * N:(t + 1) * N], in_=dj[:])

@@ -16,13 +16,12 @@ B, K, N = 4096, 512, 512
 NT = B // P
 GT = 2
 NG = NT // GT
+QW = GT * P * 4
 KW = K // 2
 FLOPS = 2 * B * N * 3 * K
 
 CHUNKS = [2, 2, 2, 2, 4, 4, 4, 4, 4, 4]
 AHEAD = 7
-PINNED = True
-H_GROUPS = list(range(NG))
 
 
 def tile_updatespeaker_pc_t_kernel(tc, encoder_hidden, spk_vectors, adr_vectors, h_tilde,
@@ -39,15 +38,14 @@ def tile_updatespeaker_pc_t_kernel(tc, encoder_hidden, spk_vectors, adr_vectors,
     with ExitStack() as ctx:
         keep = ctx.enter_context(tc.tile_pool(name="keep", bufs=1))
         wgrp_pool = ctx.enter_context(tc.tile_pool(name="wgrp", bufs=3))
-        grp_pool = ctx.enter_context(tc.tile_pool(name="grp", bufs=6))
-        cod_pool = ctx.enter_context(tc.tile_pool(name="cod", bufs=6))
+        grp_pool = ctx.enter_context(tc.tile_pool(name="grp", bufs=3))
+        cod_pool = ctx.enter_context(tc.tile_pool(name="cod", bufs=3))
         z_pool = ctx.enter_context(tc.tile_pool(name="zp", bufs=3))
         d_pool = ctx.enter_context(tc.tile_pool(name="dp", bufs=8))
         tp_pool = ctx.enter_context(tc.psum_pool(name="tp", bufs=3))
         v_pool = ctx.enter_context(tc.psum_pool(name="vp", bufs=2))
         h_pool = ctx.enter_context(tc.psum_pool(name="hp", bufs=3))
-        if PINNED:
-            ctx.enter_context(tc.manual_schedule())
+        ctx.enter_context(tc.manual_schedule())
 
         warm_in = keep.tile([P, 1], F32, name="warm_in")
         warm_out = keep.tile([P, 1], F32, name="warm_out")
@@ -103,7 +101,7 @@ def tile_updatespeaker_pc_t_kernel(tc, encoder_hidden, spk_vectors, adr_vectors,
             by_half = grp[:].bitcast(F32).rearrange("p (r h j u) -> p h r j u", h=2, j=2, u=2)
             for half in range(2):
                 bank = transpose_pair(wraw[w][:, half * 2 * K:(half + 1) * 2 * K])
-                evacuate("act" if w == 1 else "dve", by_half[:, half], bank[:].rearrange("p j u r -> p r j u"))
+                evacuate("act", by_half[:, half], bank[:].rearrange("p j u r -> p r j u"))
 
         def weight_quantise(w):
             codes = keep.tile([P, N], U32, name="wcod%d" % w, align_bytes=64)
@@ -116,16 +114,24 @@ def tile_updatespeaker_pc_t_kernel(tc, encoder_hidden, spk_vectors, adr_vectors,
 
         def act_transposes(g, a):
             bank = transpose_pair(act_cols(a, g * GT, GT))
-            grp = grp_pool.tile([P, GT * P * 4], BF16, name="grp", tag="grp", align_bytes=64)
-            evacuate("act", grp[:].bitcast(F32).rearrange("p (j r u) -> p j r u", j=GT, u=2),
+            if a == 0:
+                grp_tiles[(g, 0)] = grp_pool.tile([P, 2 * QW], BF16, name="grp2", tag="grp2", align_bytes=64)
+            elif a == 2:
+                grp_tiles[(g, 2)] = grp_pool.tile([P, QW], BF16, name="grp1", tag="grp1", align_bytes=64)
+            dst = grp_tiles[(g, a // 2 * 2)][:, a % 2 * QW:(a % 2 + 1) * QW]
+            evacuate("act", dst.bitcast(F32).rearrange("p (j r u) -> p j r u", j=GT, u=2),
                      bank[:].rearrange("p j u r -> p j r u"))
-            grp_tiles[(g, a)] = grp
 
         def act_quantise(g, a):
-            codes = cod_pool.tile([P, GT * P], U32, name="cod", tag="cod", align_bytes=64)
-            scales = cod_pool.tile([P, GT * P], U8, name="scl", tag="scl", align_bytes=64)
+            if a == 1:
+                return
+            n = 2 if a == 0 else 1
+            codes = cod_pool.tile([P, n * GT * P], U32, name="cod", tag="cod%d" % n, align_bytes=64)
+            scales = cod_pool.tile([P, n * GT * P], U8, name="scl", tag="scl%d" % n, align_bytes=64)
             nc.vector.quantize_mx(out=codes[:].bitcast(FP8X4), scales=scales[:], in_=grp_tiles[(g, a)][:])
-            cod_tiles[(g, a)] = (codes, scales)
+            for k in range(n):
+                cols = slice(k * GT * P, (k + 1) * GT * P)
+                cod_tiles[(g, a + k)] = (codes[:, cols], scales[:, cols])
 
         hb_tiles, v_tiles, z_tiles, d_tiles = {}, {}, {}, {}
 
@@ -150,7 +156,7 @@ def tile_updatespeaker_pc_t_kernel(tc, encoder_hidden, spk_vectors, adr_vectors,
                 v_tiles[(g, j)] = v
 
         def hs_operand(g):
-            return hb_tiles[g][:] if g in H_GROUPS else act_cols(1, g * GT, GT)
+            return hb_tiles[g][:]
 
         def difference(g):
             d = d_pool.tile([P, GT * N], F32, name="d", tag="d")
@@ -164,8 +170,7 @@ def tile_updatespeaker_pc_t_kernel(tc, encoder_hidden, spk_vectors, adr_vectors,
             z_tiles[g] = z
 
         def scale_difference(g):
-            eng = nc.gpsimd if g in H_GROUPS else nc.vector
-            eng.tensor_tensor(out=d_tiles[g][:], in0=z_tiles[g][:], in1=d_tiles[g][:], op=ALU.mult)
+            nc.gpsimd.tensor_tensor(out=d_tiles[g][:], in0=z_tiles[g][:], in1=d_tiles[g][:], op=ALU.mult)
 
         def finish(g):
             d = d_tiles[g]

@@ -41,7 +41,7 @@ def tile_updatespeaker_pc_t_kernel(tc, encoder_hidden, spk_vectors, adr_vectors,
         grp_pool = ctx.enter_context(tc.tile_pool(name="grp", bufs=3))
         cod_pool = ctx.enter_context(tc.tile_pool(name="cod", bufs=3))
         z_pool = ctx.enter_context(tc.tile_pool(name="zp", bufs=3))
-        d_pool = ctx.enter_context(tc.tile_pool(name="dp", bufs=8))
+        d_pool = ctx.enter_context(tc.tile_pool(name="dp", bufs=4))
         tp_pool = ctx.enter_context(tc.psum_pool(name="tp", bufs=3))
         v_pool = ctx.enter_context(tc.psum_pool(name="vp", bufs=2))
         h_pool = ctx.enter_context(tc.psum_pool(name="hp", bufs=3))
@@ -158,9 +158,16 @@ def tile_updatespeaker_pc_t_kernel(tc, encoder_hidden, spk_vectors, adr_vectors,
         def hs_operand(g):
             return hb_tiles[g][:]
 
-        def difference(g):
+        def d_tile(g):
+            c = chunk_of_tile[g * GT]
+            if CHUNKS[c] == 2 * GT:
+                return act_tiles[(0 if g * GT == chunk_start[c] else 2, c)][:].bitcast(F32)
             d = d_pool.tile([P, GT * N], F32, name="d", tag="d")
-            nc.vector.tensor_tensor(out=d[:], in0=act_cols(3, g * GT, GT), in1=hs_operand(g), op=ALU.subtract)
+            return d[:]
+
+        def difference(g):
+            d = d_tile(g)
+            nc.vector.tensor_tensor(out=d, in0=act_cols(3, g * GT, GT), in1=hs_operand(g), op=ALU.subtract)
             d_tiles[g] = d
 
         def gate(g):
@@ -170,20 +177,21 @@ def tile_updatespeaker_pc_t_kernel(tc, encoder_hidden, spk_vectors, adr_vectors,
             z_tiles[g] = z
 
         def scale_difference(g):
-            nc.gpsimd.tensor_tensor(out=d_tiles[g][:], in0=z_tiles[g][:], in1=d_tiles[g][:], op=ALU.mult)
+            nc.gpsimd.tensor_tensor(out=d_tiles[g], in0=z_tiles[g][:], in1=d_tiles[g], op=ALU.mult)
 
         def finish(g):
             d = d_tiles[g]
-            nc.vector.tensor_tensor(out=d[:], in0=d[:], in1=hs_operand(g), op=ALU.add)
+            nc.vector.tensor_tensor(out=d, in0=d, in1=hs_operand(g), op=ALU.add)
             dst = out.rearrange("(p t) n -> p (t n)", t=NT)
-            nc.sync.dma_start(out=dst[:, g * GT * N:(g + 1) * GT * N], in_=d[:])
+            nc.sync.dma_start(out=dst[:, g * GT * N:(g + 1) * GT * N], in_=d)
 
         def last_group_by_tile(g):
             dst = out.rearrange("(p t) n -> p (t n)", t=NT)
             parts = []
+            room = d_tile(g)
             for j in range(GT):
-                dj = d_pool.tile([P, N], F32, name="d", tag="d")
-                nc.vector.tensor_tensor(out=dj[:], in0=act_cols(3, g * GT + j, 1), in1=hb_tiles[g][:, j * N:(j + 1) * N],
+                dj = room[:, j * N:(j + 1) * N]
+                nc.vector.tensor_tensor(out=dj, in0=act_cols(3, g * GT + j, 1), in1=hb_tiles[g][:, j * N:(j + 1) * N],
                                         op=ALU.subtract)
                 parts.append(dj)
             zs = []
@@ -191,14 +199,14 @@ def tile_updatespeaker_pc_t_kernel(tc, encoder_hidden, spk_vectors, adr_vectors,
                 zj = z_pool.tile([P, N], F32, name="z", tag="z")
                 nc.scalar.activation(out=zj[:], in_=v_tiles[(g, j)][:], func=ACT.Sigmoid)
                 zs.append(zj)
-            nc.gpsimd.tensor_tensor(out=parts[0][:], in0=zs[0][:], in1=parts[0][:], op=ALU.mult)
+            nc.gpsimd.tensor_tensor(out=parts[0], in0=zs[0][:], in1=parts[0], op=ALU.mult)
             finish(g - 1)
-            nc.vector.tensor_tensor(out=parts[1][:], in0=zs[1][:], in1=parts[1][:], op=ALU.mult)
+            nc.vector.tensor_tensor(out=parts[1], in0=zs[1][:], in1=parts[1], op=ALU.mult)
             for j in range(GT):
                 dj = parts[j]
-                nc.vector.tensor_tensor(out=dj[:], in0=dj[:], in1=hb_tiles[g][:, j * N:(j + 1) * N], op=ALU.add)
+                nc.vector.tensor_tensor(out=dj, in0=dj, in1=hb_tiles[g][:, j * N:(j + 1) * N], op=ALU.add)
                 t = g * GT + j
-                nc.sync.dma_start(out=dst[:, t * N:(t + 1) * N], in_=dj[:])
+                nc.sync.dma_start(out=dst[:, t * N:(t + 1) * N], in_=dj)
 
         load_order = []
         for c in range(len(CHUNKS)):

@@ -21,7 +21,7 @@ KW = K // 2
 FLOPS = 2 * B * N * 3 * K
 
 CHUNKS = [2, 2, 2, 2, 4, 4, 4, 4, 4, 4]
-AHEAD = 7
+AHEAD = NG
 
 
 def tile_updatespeaker_pc_t_kernel(tc, encoder_hidden, spk_vectors, adr_vectors, h_tilde,

@@ -20,7 +20,7 @@ QW = GT * P * 4
 KW = K // 2
 FLOPS = 2 * B * N * 3 * K
 
-CHUNKS = [2, 2, 2, 2, 4, 4, 4, 4, 4, 4]
+CHUNKS = [2, 2, 2, 2, 4, 4, 8, 8]
 AHEAD = NG
 
 
@@ -160,8 +160,8 @@ def tile_updatespeaker_pc_t_kernel(tc, encoder_hidden, spk_vectors, adr_vectors,
 
         def d_tile(g):
             c = chunk_of_tile[g * GT]
-            if CHUNKS[c] == 2 * GT:
-                return act_tiles[(0 if g * GT == chunk_start[c] else 2, c)][:].bitcast(F32)
+            if CHUNKS[c] >= 2 * GT:
+                return act_cols(0 if g % 2 == 0 else 2, g // 2 * 2 * GT, 2 * GT).bitcast(F32)
             d = d_pool.tile([P, GT * N], F32, name="d", tag="d")
             return d[:]
 
@@ -210,9 +210,11 @@ def tile_updatespeaker_pc_t_kernel(tc, encoder_hidden, spk_vectors, adr_vectors,
 
         load_order = []
         for c in range(len(CHUNKS)):
+            if CHUNKS[c] > GT:
+                load_order.append((3, c - 1))
             for a in range(3):
                 load_order.append((a, c))
-            if c >= 1:
+            if c >= 1 and CHUNKS[c] == GT:
                 load_order.append((3, c - 1))
         load_order.append((3, len(CHUNKS) - 1))
         issued = [0]

from contextlib import ExitStack

import concourse.mybir as mybir
from concourse.masks import make_identity

F32 = mybir.dt.float32
BF16 = mybir.dt.bfloat16
U32 = mybir.dt.uint32
U8 = mybir.dt.uint8
FP8X4 = mybir.dt.float8_e4m3fn_x4
ALU = mybir.AluOpType
ACT = mybir.ActivationFunctionType

P = 128
B, K, N = 4096, 512, 512
NT = B // P
GT = 2
NG = NT // GT
QW = GT * P * 4
KW = K // 2
FLOPS = 2 * B * N * 3 * K

CHUNKS = [2, 2, 2, 2, 4, 4, 8, 8]
AHEAD = NG


def tile_updatespeaker_pc_t_kernel(tc, encoder_hidden, spk_vectors, adr_vectors, h_tilde,
                                              WA_xz, WA_hz, VA_hz, out):
    nc = tc.nc
    acts = [encoder_hidden, spk_vectors, adr_vectors, h_tilde]
    weights = [WA_xz, WA_hz, VA_hz]
    chunk_start = [sum(CHUNKS[:c]) for c in range(len(CHUNKS))]
    chunk_of_tile = {}
    for c, n in enumerate(CHUNKS):
        for t in range(chunk_start[c], chunk_start[c] + n):
            chunk_of_tile[t] = c

    with ExitStack() as ctx:
        keep = ctx.enter_context(tc.tile_pool(name="keep", bufs=1))
        wgrp_pool = ctx.enter_context(tc.tile_pool(name="wgrp", bufs=3))
        grp_pool = ctx.enter_context(tc.tile_pool(name="grp", bufs=3))
        cod_pool = ctx.enter_context(tc.tile_pool(name="cod", bufs=3))
        z_pool = ctx.enter_context(tc.tile_pool(name="zp", bufs=3))
        d_pool = ctx.enter_context(tc.tile_pool(name="dp", bufs=4))
        tp_pool = ctx.enter_context(tc.psum_pool(name="tp", bufs=3))
        v_pool = ctx.enter_context(tc.psum_pool(name="vp", bufs=2))
        h_pool = ctx.enter_context(tc.psum_pool(name="hp", bufs=3))
        ctx.enter_context(tc.manual_schedule())

        warm_in = keep.tile([P, 1], F32, name="warm_in")
        warm_out = keep.tile([P, 1], F32, name="warm_out")
        nc.vector.memset(warm_in[:], 0.0)
        nc.scalar.activation(out=warm_out[:], in_=warm_in[:], func=ACT.Sigmoid)
        ident_f = keep.tile([P, P], F32, name="ident_f")
        make_identity(nc, ident_f[:])
        ident_b = keep.tile([P, P], BF16, name="ident_b")
        make_identity(nc, ident_b[:])

        act_tiles = {}

        def load_chunk(a, c):
            n = CHUNKS[c]
            t0 = chunk_start[c]
            sb = keep.tile([P, n * K], BF16, name="in%d_%d" % (a, c))
            src = acts[a].rearrange("(p t) k -> p (t k)", t=NT)
            nc.sync.dma_start(out=sb[:], in_=src[:, t0 * K:(t0 + n) * K])
            act_tiles[(a, c)] = sb

        def act_cols(a, t, n_tiles):
            c = chunk_of_tile[t]
            off = (t - chunk_start[c]) * K
            return act_tiles[(a, c)][:, off:off + n_tiles * K]

        wraw = []

        def load_weight(w):
            sb = keep.tile([P, 4 * K], BF16, name="wraw%d" % w)
            nc.sync.dma_start(out=sb[:], in_=weights[w].rearrange("(p j) k -> p (j k)", j=4))
            wraw.append(sb)

        def transpose_pair(src2):
            words = src2.bitcast(F32)
            bank = tp_pool.tile([P, GT, 2, P], F32, name="bank", tag="bank")
            for j in range(GT):
                for u in range(2):
                    lo = j * KW + u * P
                    nc.tensor.transpose(bank[:, j, u, :], words[:, lo:lo + P], ident_f[:])
            return bank

        def evacuate(engine, dst, src):
            if engine == "act":
                nc.scalar.copy(out=dst, in_=src)
            else:
                nc.vector.tensor_copy(out=dst, in_=src)

        w_codes, w_scales, w_grp = [], [], []

        def weight_transposes(w):
            grp = wgrp_pool.tile([P, 4 * N], BF16, name="wgrp", tag="wgrp", align_bytes=64)
            w_grp.append(grp)
            by_half = grp[:].bitcast(F32).rearrange("p (r h j u) -> p h r j u", h=2, j=2, u=2)
            for half in range(2):
                bank = transpose_pair(wraw[w][:, half * 2 * K:(half + 1) * 2 * K])
                evacuate("act", by_half[:, half], bank[:].rearrange("p j u r -> p r j u"))

        def weight_quantise(w):
            codes = keep.tile([P, N], U32, name="wcod%d" % w, align_bytes=64)
            scales = keep.tile([P, N], U8, name="wscl%d" % w, align_bytes=64)
            nc.vector.quantize_mx(out=codes[:].bitcast(FP8X4), scales=scales[:], in_=w_grp[w][:])
            w_codes.append(codes)
            w_scales.append(scales)

        grp_tiles, cod_tiles = {}, {}

        def act_transposes(g, a):
            bank = transpose_pair(act_cols(a, g * GT, GT))
            if a == 0:
                grp_tiles[(g, 0)] = grp_pool.tile([P, 2 * QW], BF16, name="grp2", tag="grp2", align_bytes=64)
            elif a == 2:
                grp_tiles[(g, 2)] = grp_pool.tile([P, QW], BF16, name="grp1", tag="grp1", align_bytes=64)
            dst = grp_tiles[(g, a // 2 * 2)][:, a % 2 * QW:(a % 2 + 1) * QW]
            evacuate("act", dst.bitcast(F32).rearrange("p (j r u) -> p j r u", j=GT, u=2),
                     bank[:].rearrange("p j u r -> p j r u"))

        def act_quantise(g, a):
            if a == 1:
                return
            n = 2 if a == 0 else 1
            codes = cod_pool.tile([P, n * GT * P], U32, name="cod", tag="cod%d" % n, align_bytes=64)
            scales = cod_pool.tile([P, n * GT * P], U8, name="scl", tag="scl%d" % n, align_bytes=64)
            nc.vector.quantize_mx(out=codes[:].bitcast(FP8X4), scales=scales[:], in_=grp_tiles[(g, a)][:])
            for k in range(n):
                cols = slice(k * GT * P, (k + 1) * GT * P)
                cod_tiles[(g, a + k)] = (codes[:, cols], scales[:, cols])

        hb_tiles, v_tiles, z_tiles, d_tiles = {}, {}, {}, {}

        def hs_to_psum(g, j):
            if j == 0:
                hb = h_pool.tile([P, GT * N], BF16, name="hb", tag="hb")
                hb_tiles[g] = hb
            nc.tensor.matmul(hb_tiles[g][:, j * N:(j + 1) * N], lhsT=ident_b[:], rhs=act_cols(1, g * GT + j, 1),
                             start=True, stop=True)

        def products(g):
            for j in range(GT):
                v = v_pool.tile([P, N], F32, name="v", tag="v")
                for a in range(3):
                    codes, scales = cod_tiles[(g, a)]
                    nc.tensor.matmul_mx(out=v[:],
                                        lhsT=codes[:, j * P:(j + 1) * P].bitcast(FP8X4),
                                        lhsT_scale=scales[:, j * P:(j + 1) * P],
                                        rhs=w_codes[a][:].bitcast(FP8X4),
                                        rhs_scale=w_scales[a][:],
                                        start=(a == 0), stop=(a == 2))
                v_tiles[(g, j)] = v

        def hs_operand(g):
            return hb_tiles[g][:]

        def d_tile(g):
            c = chunk_of_tile[g * GT]
            if CHUNKS[c] >= 2 * GT:
                return act_cols(0 if g % 2 == 0 else 2, g // 2 * 2 * GT, 2 * GT).bitcast(F32)
            d = d_pool.tile([P, GT * N], F32, name="d", tag="d")
            return d[:]

        def difference(g):
            d = d_tile(g)
            nc.vector.tensor_tensor(out=d, in0=act_cols(3, g * GT, GT), in1=hs_operand(g), op=ALU.subtract)
            d_tiles[g] = d

        def gate(g):
            z = z_pool.tile([P, GT * N], F32, name="z", tag="z")
            for j in range(GT):
                nc.scalar.activation(out=z[:, j * N:(j + 1) * N], in_=v_tiles[(g, j)][:], func=ACT.Sigmoid)
            z_tiles[g] = z

        def scale_difference(g):
            nc.gpsimd.tensor_tensor(out=d_tiles[g], in0=z_tiles[g][:], in1=d_tiles[g], op=ALU.mult)

        def finish(g):
            d = d_tiles[g]
            nc.vector.tensor_tensor(out=d, in0=d, in1=hs_operand(g), op=ALU.add)
            dst = out.rearrange("(p t) n -> p (t n)", t=NT)
            nc.sync.dma_start(out=dst[:, g * GT * N:(g + 1) * GT * N], in_=d)

        def last_group_by_tile(g):
            dst = out.rearrange("(p t) n -> p (t n)", t=NT)
            parts = []
            room = d_tile(g)
            for j in range(GT):
                dj = room[:, j * N:(j + 1) * N]
                nc.vector.tensor_tensor(out=dj, in0=act_cols(3, g * GT + j, 1), in1=hb_tiles[g][:, j * N:(j + 1) * N],
                                        op=ALU.subtract)
                parts.append(dj)
            zs = []
            for j in range(GT):
                zj = z_pool.tile([P, N], F32, name="z", tag="z")
                nc.scalar.activation(out=zj[:], in_=v_tiles[(g, j)][:], func=ACT.Sigmoid)
                zs.append(zj)
            nc.gpsimd.tensor_tensor(out=parts[0], in0=zs[0][:], in1=parts[0], op=ALU.mult)
            finish(g - 1)
            nc.vector.tensor_tensor(out=parts[1], in0=zs[1][:], in1=parts[1], op=ALU.mult)
            for j in range(GT):
                dj = parts[j]
                nc.vector.tensor_tensor(out=dj, in0=dj, in1=hb_tiles[g][:, j * N:(j + 1) * N], op=ALU.add)
                t = g * GT + j
                nc.sync.dma_start(out=dst[:, t * N:(t + 1) * N], in_=dj)

        load_order = []
        for c in range(len(CHUNKS)):
            if CHUNKS[c] > GT:
                load_order.append((3, c - 1))
            for a in range(3):
                load_order.append((a, c))
            if c >= 1 and CHUNKS[c] == GT:
                load_order.append((3, c - 1))
        load_order.append((3, len(CHUNKS) - 1))
        issued = [0]

        def issue_loads_up_to(g):
            while issued[0] < len(load_order):
                a, c = load_order[issued[0]]
                if chunk_start[c] > g * GT:
                    break
                load_chunk(a, c)
                issued[0] += 1

        for w in range(3):
            load_weight(w)
        issue_loads_up_to(AHEAD - 1)
        for w in range(3):
            weight_transposes(w)
            weight_quantise(w)
        for a in range(3):
            act_transposes(0, a)
        for a in range(3):
            act_quantise(0, a)

        hs_to_psum(0, 0)
        for i in range(NG - 1):
            issue_loads_up_to(i + AHEAD)
            for a in range(3):
                act_transposes(i + 1, a)
            hs_to_psum(i, 1)
            products(i)
            hs_to_psum(i + 1, 0)
            difference(i)
            for a in range(3):
                act_quantise(i + 1, a)
            gate(i)
            if i >= 1:
                finish(i - 1)
            scale_difference(i)
        hs_to_psum(NG - 1, 1)
        products(NG - 1)
        last_group_by_tile(NG - 1)
